import numpy as np
import ml_dtypes


def mxq(x, axis, fmt="e4m3"):
    dtype, down = {"e4m3": (ml_dtypes.float8_e4m3fn, 7), "e5m2": (ml_dtypes.float8_e5m2, 14)}[fmt]
    v = np.moveaxis(np.asarray(x, np.float32).astype(ml_dtypes.bfloat16).astype(np.float64), axis, -1)
    blocks = v.reshape(v.shape[:-1] + (-1, 32))
    amax = np.abs(blocks).max(-1, keepdims=True)
    byte = np.maximum(np.where(amax > 0, np.frexp(amax)[1] - 1 + 127, 0) - down, 1)
    scale = np.exp2(byte - 127.0)
    codes = (blocks / scale).astype(np.float32).astype(dtype).astype(np.float64)
    return np.moveaxis((codes * scale).reshape(v.shape), -1, axis)


WIDE = False


def mx_kscale(k):
    if not WIDE:
        return np.ones(k)
    levels = np.array([10, -10, 5, -5, 0])
    if k % 512:
        return np.exp2(np.random.permutation(np.resize(levels, k // 32))).repeat(32)
    a = np.empty((k // 512, 16))
    for p in range(k // 512):
        a[p, :8] = np.random.permutation(np.resize(levels, 8))
        for g in range(8):
            far = levels[np.abs(levels - a[p, g]) >= 10]
            a[p, g + 8] = far[np.random.randint(len(far))]
    return np.exp2(a.ravel()).repeat(32)


BF16 = ml_dtypes.bfloat16


def bf(x):
    return np.asarray(x, np.float32).astype(BF16)


def f64(x):
    return np.asarray(x).astype(np.float64)


B, S, C, HD = 4, 1024, 1024, 128
H = C // HD
HP = HD // 2
EPS = 1e-6
THETA = 10000.0


def rmsnorm(h, g):
    return h * (1.0 / np.sqrt(np.mean(h * h, axis=-1, keepdims=True) + EPS)) * g


def apply_rope1(h, freqs):
    sh = h.shape
    h_ = h.reshape(*sh[:-1], -1, 1, 2)
    out = freqs[..., 0] * h_[..., 0] + freqs[..., 1] * h_[..., 1]
    return out.reshape(sh)


def setup_inputs():
    s = mx_kscale(C)
    pos = f64(np.random.randint(0, S, size=(S, 1)))
    inv_freq = 1.0 / THETA ** (np.arange(HP) / HP)
    ang = pos * inv_freq
    cos, sin = np.cos(ang), np.sin(ang)
    rot = np.stack([np.stack([cos, -sin], -1), np.stack([sin, cos], -1)], -2)
    return {"x": bf(np.random.standard_normal((B, S, C)) * s),
            "freqs": bf(rot[None, :, None]),
            "w": bf(np.random.standard_normal((C, C)) / np.sqrt(C) / s[None, :]),
            "b": bf(np.random.standard_normal(C) * 0.3),
            "g": bf(1.0 + 0.1 * np.random.standard_normal(HD))}


def reference(x, freqs, w, b, g):
    p = (mxq(f64(x), 2, "e4m3") @ mxq(f64(w), 1, "e4m3").T) + f64(b)
    h = p.reshape(B, S, H, HD)
    return apply_rope1(rmsnorm(h, f64(g)), f64(freqs))

@@ -1,0 +1,268 @@
+from contextlib import ExitStack
+
+import concourse.mybir as mybir
+from concourse.masks import make_identity
+
+F32 = mybir.dt.float32
+BF16 = mybir.dt.bfloat16
+U32 = mybir.dt.uint32
+U8 = mybir.dt.uint8
+FP8X4 = mybir.dt.float8_e4m3fn_x4
+ACT = mybir.ActivationFunctionType
+ALU = mybir.AluOpType
+
+P = 128
+K = 1024
+K_PASSES = 2
+WORDS_PER_PASS = 256
+HEADS = 8
+HEAD_DIM = 128
+PAIRS = HEAD_DIM // 2
+EPS = 1e-6
+TOKENS = 4096
+GROUP = 512
+GROUPS = TOKENS // GROUP
+TILES = GROUP // P
+ALL_TILES = GROUPS * TILES
+SEQ_HALVES = 2
+BLOCK_ROWS = 256
+BLOCKS_PER_GROUP = (GROUP // BLOCK_ROWS) * K_PASSES
+X_BLOCKS = GROUPS * BLOCKS_PER_GROUP
+W_CHUNKS = HEADS * HEAD_DIM // BLOCK_ROWS
+BANK_HEADS = 4
+PROJECT_AHEAD = TILES
+QUANTISE_AHEAD = 10
+
+FLOPS = 2 * TOKENS * K * HEADS * HEAD_DIM
+
+
+def tile_selfattention_pa_t_kernel(tc, x, freqs, w, b, g, out):
+    nc = tc.nc
+    x_groups = x.rearrange("n s k -> (n s) k").rearrange("(a q t) k -> a q t k", q=P, t=TILES)
+    out_tiles = out.rearrange("n s h d -> (n s) (h d)").rearrange("(a q t) f -> a t q f", q=P, t=TILES)
+    w_chunks = w.rearrange("(c r q) k -> c q r k", r=2, q=P)
+    freqs_rows = freqs.rearrange("a s b j r i -> (a s b) (j r i)").rearrange(
+        "(e q t) f -> q e t f", q=P, t=TILES
+    )
+
+    with ExitStack() as ctx:
+        keep = ctx.enter_context(tc.tile_pool(name="keep", bufs=1))
+        x_grouped_pool = ctx.enter_context(tc.tile_pool(name="x_grouped_pool", bufs=2))
+        w_grouped_pool = ctx.enter_context(tc.tile_pool(name="w_grouped_pool", bufs=2))
+        x_mx_pool = ctx.enter_context(tc.tile_pool(name="x_mx_pool", bufs=3))
+        biased_pool = ctx.enter_context(tc.tile_pool(name="biased_pool", bufs=2 * HEADS))
+        small_pool = ctx.enter_context(tc.tile_pool(name="small_pool", bufs=4))
+        prod_pool = ctx.enter_context(tc.tile_pool(name="prod_pool", bufs=4))
+        result_pool = ctx.enter_context(tc.tile_pool(name="result_pool", bufs=3))
+        acc_psum = ctx.enter_context(tc.psum_pool(name="acc_psum", bufs=2))
+        turned_psum = ctx.enter_context(tc.psum_pool(name="turned_psum", bufs=6))
+        ctx.enter_context(tc.manual_schedule())
+
+        x_sb = keep.tile([P, GROUPS, TILES, K], BF16, name="x_sb")
+        w_sb = keep.tile([P, HEADS, K], BF16, name="w_sb")
+        b_rows_bf = keep.tile([HEADS, HEAD_DIM], BF16, name="b_rows_bf")
+        g_all = keep.tile([P, HEAD_DIM], BF16, name="g_all")
+        freqs_sb = keep.tile([P, SEQ_HALVES, TILES, 4 * PAIRS], BF16, name="freqs_sb")
+        nc.sync.dma_start(out=b_rows_bf[:], in_=b.rearrange("(h d) -> h d", d=HEAD_DIM))
+        nc.sync.dma_start(out=x_sb[:, 0, 0:2], in_=x_groups[0][:, 0:2])
+        nc.sync.dma_start(out=x_sb[:, 0, 2:4], in_=x_groups[0][:, 2:4])
+        nc.sync.dma_start(out=w_sb[:, 0:2, :], in_=w_chunks[0])
+        nc.sync.dma_start(out=x_sb[:, 1], in_=x_groups[1])
+        for c in range(1, W_CHUNKS):
+            nc.sync.dma_start(out=w_sb[:, 2 * c : 2 * c + 2, :], in_=w_chunks[c])
+        nc.sync.dma_start(out=g_all[:], in_=g.partition_broadcast(P))
+        nc.sync.dma_start(out=freqs_sb[:], in_=freqs_rows)
+        for a in range(2, GROUPS):
+            nc.sync.dma_start(out=x_sb[:, a], in_=x_groups[a])
+
+        ident = keep.tile([P, P], F32, name="ident")
+        make_identity(nc, ident[:])
+        sort_pairs = keep.tile([P, P], F32, name="sort_pairs")
+        nc.vector.tensor_copy(
+            out=sort_pairs[:].rearrange("q (i j) -> q i j", i=2), in_=ident[:].rearrange("q (j i) -> q i j", i=2)
+        )
+
+        b_rows = keep.tile([P, P], F32, name="b_rows")
+        nc.vector.memset(b_rows[:], 0.0)
+        nc.vector.tensor_copy(out=b_rows[0:HEADS, :], in_=b_rows_bf[:])
+        b_turned = turned_psum.tile([P, P], F32, name="b_turned", tag="turned")
+        nc.tensor.transpose(b_turned[:], b_rows[:], ident[:])
+        b_col = keep.tile([P, HEADS], F32, name="b_col")
+        nc.vector.tensor_copy(out=b_col[:], in_=b_turned[:, 0:HEADS])
+
+        def transpose_block(rows, k_pass, grouped):
+            words = turned_psum.tile([P, 2, BLOCK_ROWS], F32, name="words", tag="turned")
+            for u in range(2):
+                first = WORDS_PER_PASS * k_pass
+                for r in range(2):
+                    nc.tensor.transpose(
+                        words[:, u, P * r : P * (r + 1)],
+                        rows[:, r, :].bitcast(F32)[:, first + u : first + WORDS_PER_PASS : 2],
+                        ident[:],
+                    )
+            copy_out = nc.scalar.copy if k_pass == 0 else nc.vector.tensor_copy
+            copy_out(
+                out=grouped.bitcast(F32).rearrange("q (n u) -> q n u", u=2),
+                in_=words[:].rearrange("q u n -> q n u"),
+            )
+
+        x_grouped = {}
+        x_codes = {}
+        x_scales = {}
+
+        def prepare_x_block(block):
+            group, rest = divmod(block, BLOCKS_PER_GROUP)
+            half, k_pass = divmod(rest, K_PASSES)
+            if rest == 0:
+                x_grouped[group] = x_grouped_pool.tile(
+                    [P, K_PASSES, GROUP // BLOCK_ROWS, 4 * BLOCK_ROWS], BF16, name="x_grouped", align_bytes=64
+                )
+                x_codes[group] = x_mx_pool.tile([P, K_PASSES, GROUP], U32, name="x_codes", align_bytes=64)
+                x_scales[group] = x_mx_pool.tile([P, K_PASSES, GROUP], U8, name="x_scales", align_bytes=64)
+            transpose_block(x_sb[:, group, 2 * half : 2 * half + 2, :], k_pass, x_grouped[group][:, k_pass, half, :])
+
+        def quantise_x_group(group):
+            nc.vector.quantize_mx(
+                out=x_codes[group][:].rearrange("q c n -> q (c n)").bitcast(FP8X4),
+                scales=x_scales[group][:].rearrange("q c n -> q (c n)"),
+                in_=x_grouped[group][:].rearrange("q c e n -> q (c e n)"),
+            )
+
+        w_codes = keep.tile([P, W_CHUNKS, K_PASSES, BLOCK_ROWS], U32, name="w_codes", align_bytes=64)
+        w_scales = keep.tile([P, W_CHUNKS, K_PASSES, BLOCK_ROWS], U8, name="w_scales", align_bytes=64)
+
+        def quantise_w_chunk(c):
+            w_grouped = w_grouped_pool.tile([P, K_PASSES, 4 * BLOCK_ROWS], BF16, name="w_grouped", align_bytes=64)
+            for k_pass in range(K_PASSES):
+                transpose_block(w_sb[:, 2 * c : 2 * c + 2, :], k_pass, w_grouped[:, k_pass, :])
+            nc.vector.quantize_mx(
+                out=w_codes[:, c].rearrange("q c n -> q (c n)").bitcast(FP8X4),
+                scales=w_scales[:, c].rearrange("q c n -> q (c n)"),
+                in_=w_grouped[:].rearrange("q c n -> q (c n)"),
+            )
+
+        for block in range(QUANTISE_AHEAD - PROJECT_AHEAD):
+            prepare_x_block(block)
+            if block == BLOCKS_PER_GROUP - 1:
+                quantise_x_group(0)
+        quantise_w_chunk(0)
+
+        matrices = keep.tile([P, SEQ_HALVES, TILES, 2, PAIRS, 2], F32, name="matrices")
+
+        for e in range(SEQ_HALVES):
+            for t in range(TILES):
+                nc.gpsimd.tensor_tensor(
+                    out=matrices[:, e, t],
+                    in0=freqs_sb[:, e, t, :].rearrange("q (j r i) -> q i j r", r=2, i=2),
+                    in1=g_all[:].rearrange("q (j i) -> q i j", i=2).unsqueeze(3).to_broadcast([P, 2, PAIRS, 2]),
+                    op=ALU.mult,
+                )
+
+        biased = {}
+
+        def project(group, head):
+            acc = acc_psum.tile([P, GROUP], F32, name="acc")
+            chunk, place = divmod(head, 2)
+            feats = slice(HEAD_DIM * place, HEAD_DIM * (place + 1))
+            for k_pass in range(K_PASSES):
+                nc.tensor.matmul_mx(
+                    out=acc[:],
+                    lhsT=w_codes[:, chunk, k_pass, feats].bitcast(FP8X4),
+                    lhsT_scale=w_scales[:, chunk, k_pass, feats],
+                    rhs=x_codes[group][:, k_pass, :].bitcast(FP8X4),
+                    rhs_scale=x_scales[group][:, k_pass, :],
+                    start=(k_pass == 0),
+                    stop=(k_pass == K_PASSES - 1),
+                )
+            return acc
+
+        def add_bias(acc, group, head):
+            biased[group, head] = biased_pool.tile([P, GROUP], F32, name="biased")
+            nc.scalar.activation(
+                out=biased[group, head][:], in_=acc[:], func=ACT.Identity, bias=b_col[:, head : head + 1], scale=1.0
+            )
+
+        def turn_back(group, t, bank):
+            u = turned_psum.tile([P, BANK_HEADS, HEAD_DIM], F32, name="u", tag="turned")
+            for h in range(BANK_HEADS):
+                nc.tensor.transpose(
+                    u[:, h, :], biased[group, BANK_HEADS * bank + h][:, P * t : P * (t + 1)], sort_pairs[:]
+                )
+            return u
+
+        def sum_squares(u):
+            sums = small_pool.tile([P, BANK_HEADS], F32, name="sums")
+            squares = small_pool.tile([P, BANK_HEADS, HEAD_DIM], F32, name="squares")
+            for h in range(BANK_HEADS):
+                nc.scalar.activation(
+                    out=squares[:, h, :], in_=u[:, h, :], func=ACT.Square, accum_out=sums[:, h : h + 1]
+                )
+            return sums
+
+        def inverse_rms(sums):
+            rstd = small_pool.tile([P, BANK_HEADS], F32, name="rstd")
+            nc.scalar.activation(
+                out=rstd[:], in_=sums[:], func=ACT.Abs_reciprocal_sqrt, scale=1.0 / HEAD_DIM, bias=EPS
+            )
+            return rstd
+
+        def multiply(u, rstd, matrix):
+            prod = prod_pool.tile([P, BANK_HEADS, 2, HEAD_DIM], F32, name="prod")
+            for h in range(BANK_HEADS):
+                nc.vector.scalar_tensor_tensor(
+                    out=prod[:, h].rearrange("q i (j r) -> q (i j) r", r=2),
+                    in0=u[:, h, :].unsqueeze(2).to_broadcast([P, HEAD_DIM, 2]),
+                    scalar=rstd[:, h : h + 1],
+                    in1=matrix.rearrange("q i j r -> q (i j) r"),
+                    op0=ALU.mult,
+                    op1=ALU.mult,
+                )
+            return prod
+
+        def add_pairs(prod, result_half):
+            nc.gpsimd.tensor_tensor(
+                out=result_half.rearrange("q (h f) -> q h f", h=BANK_HEADS),
+                in0=prod[:, :, 0, :],
+                in1=prod[:, :, 1, :],
+                op=ALU.add,
+            )
+
+        bank_cols = BANK_HEADS * HEAD_DIM
+        for i in range(-PROJECT_AHEAD, ALL_TILES):
+            ahead_group, head_pair = divmod(i + PROJECT_AHEAD, TILES)
+            projecting = ahead_group < GROUPS
+            finishing = i >= 0
+            block = i + QUANTISE_AHEAD
+            group, t = divmod(i, TILES)
+
+            if not finishing and head_pair + 1 < W_CHUNKS:
+                quantise_w_chunk(head_pair + 1)
+            if finishing:
+                u_0 = turn_back(group, t, 0)
+            if projecting:
+                acc_0 = project(ahead_group, 2 * head_pair)
+            if finishing:
+                u_1 = turn_back(group, t, 1)
+            if projecting:
+                acc_1 = project(ahead_group, 2 * head_pair + 1)
+            if finishing:
+                sums_0 = sum_squares(u_0)
+            if projecting:
+                add_bias(acc_0, ahead_group, 2 * head_pair)
+            if finishing:
+                rstd_0 = inverse_rms(sums_0)
+                sums_1 = sum_squares(u_1)
+            if projecting:
+                add_bias(acc_1, ahead_group, 2 * head_pair + 1)
+            if block < X_BLOCKS:
+                prepare_x_block(block)
+            if finishing:
+                rstd_1 = inverse_rms(sums_1)
+                matrix = matrices[:, group % SEQ_HALVES, t]
+                result = result_pool.tile([P, HEADS * HEAD_DIM], F32, name="result")
+                add_pairs(multiply(u_0, rstd_0, matrix), result[:, 0:bank_cols])
+            if block < X_BLOCKS and block % BLOCKS_PER_GROUP == BLOCKS_PER_GROUP - 1:
+                quantise_x_group(block // BLOCKS_PER_GROUP)
+            if finishing:
+                add_pairs(multiply(u_1, rstd_1, matrix), result[:, bank_cols : 2 * bank_cols])
+                nc.sync.dma_start(out=out_tiles[group, t], in_=result[:])

@@ -23,15 +23,21 @@ TOKENS = 4096
 GROUP = 512
 GROUPS = TOKENS // GROUP
 TILES = GROUP // P
-ALL_TILES = GROUPS * TILES
 SEQ_HALVES = 2
 BLOCK_ROWS = 256
-BLOCKS_PER_GROUP = (GROUP // BLOCK_ROWS) * K_PASSES
+HALVES = GROUP // BLOCK_ROWS
+BLOCKS_PER_GROUP = HALVES * K_PASSES
 X_BLOCKS = GROUPS * BLOCKS_PER_GROUP
 W_CHUNKS = HEADS * HEAD_DIM // BLOCK_ROWS
 BANK_HEADS = 4
-PROJECT_AHEAD = TILES
-QUANTISE_AHEAD = 10
+BANK_COLS = BANK_HEADS * HEAD_DIM
+BANKS = HEADS // BANK_HEADS
+UNITS = GROUPS * BANKS * TILES
+PROJECT_AHEAD = 6
+BIAS_AHEAD = 5
+X_BLOCK_LEAD = 17
+X_QUANTISE_LEAD = 9
+G_ROW = HEADS
 
 FLOPS = 2 * TOKENS * K * HEADS * HEAD_DIM
 
@@ -50,30 +56,33 @@ def tile_selfattention_pa_t_kernel(tc, x, freqs, w, b, g, out):
         x_grouped_pool = ctx.enter_context(tc.tile_pool(name="x_grouped_pool", bufs=2))
         w_grouped_pool = ctx.enter_context(tc.tile_pool(name="w_grouped_pool", bufs=2))
         x_mx_pool = ctx.enter_context(tc.tile_pool(name="x_mx_pool", bufs=3))
-        biased_pool = ctx.enter_context(tc.tile_pool(name="biased_pool", bufs=2 * HEADS))
+        biased_pool = ctx.enter_context(tc.tile_pool(name="biased_pool", bufs=14))
         small_pool = ctx.enter_context(tc.tile_pool(name="small_pool", bufs=4))
         prod_pool = ctx.enter_context(tc.tile_pool(name="prod_pool", bufs=4))
-        result_pool = ctx.enter_context(tc.tile_pool(name="result_pool", bufs=3))
-        acc_psum = ctx.enter_context(tc.psum_pool(name="acc_psum", bufs=2))
-        turned_psum = ctx.enter_context(tc.psum_pool(name="turned_psum", bufs=6))
+        result_pool = ctx.enter_context(tc.tile_pool(name="result_pool", bufs=6))
+        acc_psum = ctx.enter_context(tc.psum_pool(name="acc_psum", bufs=3))
+        turned_psum = ctx.enter_context(tc.psum_pool(name="turned_psum", bufs=5))
         ctx.enter_context(tc.manual_schedule())
 
         x_sb = keep.tile([P, GROUPS, TILES, K], BF16, name="x_sb")
         w_sb = keep.tile([P, HEADS, K], BF16, name="w_sb")
-        b_rows_bf = keep.tile([HEADS, HEAD_DIM], BF16, name="b_rows_bf")
-        g_all = keep.tile([P, HEAD_DIM], BF16, name="g_all")
+        small_rows = keep.tile([HEADS + 1, HEAD_DIM], BF16, name="small_rows")
         freqs_sb = keep.tile([P, SEQ_HALVES, TILES, 4 * PAIRS], BF16, name="freqs_sb")
-        nc.sync.dma_start(out=b_rows_bf[:], in_=b.rearrange("(h d) -> h d", d=HEAD_DIM))
+        nc.scalar.dma_start(out=small_rows[0:HEADS, :], in_=b.rearrange("(h d) -> h d", d=HEAD_DIM))
+        nc.scalar.dma_start(out=small_rows[G_ROW : G_ROW + 1, :], in_=g.unsqueeze(0))
         nc.sync.dma_start(out=x_sb[:, 0, 0:2], in_=x_groups[0][:, 0:2])
-        nc.sync.dma_start(out=x_sb[:, 0, 2:4], in_=x_groups[0][:, 2:4])
         nc.sync.dma_start(out=w_sb[:, 0:2, :], in_=w_chunks[0])
-        nc.sync.dma_start(out=x_sb[:, 1], in_=x_groups[1])
-        for c in range(1, W_CHUNKS):
-            nc.sync.dma_start(out=w_sb[:, 2 * c : 2 * c + 2, :], in_=w_chunks[c])
-        nc.sync.dma_start(out=g_all[:], in_=g.partition_broadcast(P))
+        nc.sync.dma_start(out=x_sb[:, 0, 2:4], in_=x_groups[0][:, 2:4])
+        nc.sync.dma_start(out=w_sb[:, 2:4, :], in_=w_chunks[1])
         nc.sync.dma_start(out=freqs_sb[:], in_=freqs_rows)
-        for a in range(2, GROUPS):
+        for c in range(2, W_CHUNKS):
+            nc.sync.dma_start(out=w_sb[:, 2 * c : 2 * c + 2, :], in_=w_chunks[c])
+        for a in range(1, GROUPS):
             nc.sync.dma_start(out=x_sb[:, a], in_=x_groups[a])
+
+        warm = keep.tile([P, 1], F32, name="warm")
+        nc.vector.memset(warm[:], 1.0)
+        nc.scalar.activation(out=warm[:], in_=warm[:], func=ACT.Abs_reciprocal_sqrt)
 
         ident = keep.tile([P, P], F32, name="ident")
         make_identity(nc, ident[:])
@@ -81,26 +90,22 @@ def tile_selfattention_pa_t_kernel(tc, x, freqs, w, b, g, out):
         nc.vector.tensor_copy(
             out=sort_pairs[:].rearrange("q (i j) -> q i j", i=2), in_=ident[:].rearrange("q (j i) -> q i j", i=2)
         )
+        ident_bf = keep.tile([P, P], BF16, name="ident_bf")
+        nc.vector.tensor_copy(out=ident_bf[:], in_=ident[:])
 
-        b_rows = keep.tile([P, P], F32, name="b_rows")
-        nc.vector.memset(b_rows[:], 0.0)
-        nc.vector.tensor_copy(out=b_rows[0:HEADS, :], in_=b_rows_bf[:])
-        b_turned = turned_psum.tile([P, P], F32, name="b_turned", tag="turned")
-        nc.tensor.transpose(b_turned[:], b_rows[:], ident[:])
-        b_col = keep.tile([P, HEADS], F32, name="b_col")
-        nc.vector.tensor_copy(out=b_col[:], in_=b_turned[:, 0:HEADS])
-
-        def transpose_block(rows, k_pass, grouped):
+        def transpose_block(rows, k_pass):
             words = turned_psum.tile([P, 2, BLOCK_ROWS], F32, name="words", tag="turned")
+            first = WORDS_PER_PASS * k_pass
             for u in range(2):
-                first = WORDS_PER_PASS * k_pass
                 for r in range(2):
                     nc.tensor.transpose(
                         words[:, u, P * r : P * (r + 1)],
                         rows[:, r, :].bitcast(F32)[:, first + u : first + WORDS_PER_PASS : 2],
                         ident[:],
                     )
-            copy_out = nc.scalar.copy if k_pass == 0 else nc.vector.tensor_copy
+            return words
+
+        def copy_block(words, grouped, copy_out):
             copy_out(
                 out=grouped.bitcast(F32).rearrange("q (n u) -> q n u", u=2),
                 in_=words[:].rearrange("q u n -> q n u"),
@@ -110,84 +115,92 @@ def tile_selfattention_pa_t_kernel(tc, x, freqs, w, b, g, out):
         x_codes = {}
         x_scales = {}
 
+        def engine_of(k_pass):
+            return nc.scalar.copy if k_pass == 0 else nc.vector.tensor_copy
+
+        def parts_of(group):
+            return HALVES if group == 0 else 1
+
         def prepare_x_block(block):
             group, rest = divmod(block, BLOCKS_PER_GROUP)
             half, k_pass = divmod(rest, K_PASSES)
+            parts = parts_of(group)
             if rest == 0:
                 x_grouped[group] = x_grouped_pool.tile(
-                    [P, K_PASSES, GROUP // BLOCK_ROWS, 4 * BLOCK_ROWS], BF16, name="x_grouped", align_bytes=64
+                    [P, parts, K_PASSES, HALVES // parts, 4 * BLOCK_ROWS], BF16, name="x_grouped", align_bytes=64
                 )
-                x_codes[group] = x_mx_pool.tile([P, K_PASSES, GROUP], U32, name="x_codes", align_bytes=64)
-                x_scales[group] = x_mx_pool.tile([P, K_PASSES, GROUP], U8, name="x_scales", align_bytes=64)
-            transpose_block(x_sb[:, group, 2 * half : 2 * half + 2, :], k_pass, x_grouped[group][:, k_pass, half, :])
+                x_codes[group] = x_mx_pool.tile(
+                    [P, parts, K_PASSES, GROUP // parts], U32, name="x_codes", align_bytes=64
+                )
+                x_scales[group] = x_mx_pool.tile(
+                    [P, parts, K_PASSES, GROUP // parts], U8, name="x_scales", align_bytes=64
+                )
+            part, place = (half, 0) if parts == HALVES else (0, half)
+            words = transpose_block(x_sb[:, group, 2 * half : 2 * half + 2, :], k_pass)
+            return words, x_grouped[group][:, part, k_pass, place, :], engine_of(k_pass)
 
-        def quantise_x_group(group):
+        def quantise_x(group, part):
             nc.vector.quantize_mx(
-                out=x_codes[group][:].rearrange("q c n -> q (c n)").bitcast(FP8X4),
-                scales=x_scales[group][:].rearrange("q c n -> q (c n)"),
-                in_=x_grouped[group][:].rearrange("q c e n -> q (c e n)"),
+                out=x_codes[group][:, part].rearrange("q c n -> q (c n)").bitcast(FP8X4),
+                scales=x_scales[group][:, part].rearrange("q c n -> q (c n)"),
+                in_=x_grouped[group][:, part].rearrange("q c e n -> q (c e n)"),
             )
 
         w_codes = keep.tile([P, W_CHUNKS, K_PASSES, BLOCK_ROWS], U32, name="w_codes", align_bytes=64)
         w_scales = keep.tile([P, W_CHUNKS, K_PASSES, BLOCK_ROWS], U8, name="w_scales", align_bytes=64)
+        w_grouped = {}
 
-        def quantise_w_chunk(c):
-            w_grouped = w_grouped_pool.tile([P, K_PASSES, 4 * BLOCK_ROWS], BF16, name="w_grouped", align_bytes=64)
-            for k_pass in range(K_PASSES):
-                transpose_block(w_sb[:, 2 * c : 2 * c + 2, :], k_pass, w_grouped[:, k_pass, :])
+        def prepare_w_block(c, k_pass):
+            if k_pass == 0:
+                w_grouped[c] = w_grouped_pool.tile(
+                    [P, K_PASSES, 4 * BLOCK_ROWS], BF16, name="w_grouped", align_bytes=64
+                )
+            words = transpose_block(w_sb[:, 2 * c : 2 * c + 2, :], k_pass)
+            return words, w_grouped[c][:, k_pass, :], engine_of(k_pass)
+
+        def quantise_w(c):
             nc.vector.quantize_mx(
                 out=w_codes[:, c].rearrange("q c n -> q (c n)").bitcast(FP8X4),
                 scales=w_scales[:, c].rearrange("q c n -> q (c n)"),
-                in_=w_grouped[:].rearrange("q c n -> q (c n)"),
+                in_=w_grouped[c][:].rearrange("q c n -> q (c n)"),
             )
-
-        for block in range(QUANTISE_AHEAD - PROJECT_AHEAD):
-            prepare_x_block(block)
-            if block == BLOCKS_PER_GROUP - 1:
-                quantise_x_group(0)
-        quantise_w_chunk(0)
-
-        matrices = keep.tile([P, SEQ_HALVES, TILES, 2, PAIRS, 2], F32, name="matrices")
-
-        for e in range(SEQ_HALVES):
-            for t in range(TILES):
-                nc.gpsimd.tensor_tensor(
-                    out=matrices[:, e, t],
-                    in0=freqs_sb[:, e, t, :].rearrange("q (j r i) -> q i j r", r=2, i=2),
-                    in1=g_all[:].rearrange("q (j i) -> q i j", i=2).unsqueeze(3).to_broadcast([P, 2, PAIRS, 2]),
-                    op=ALU.mult,
-                )
 
         biased = {}
 
-        def project(group, head):
+        def project(job):
+            group, head = divmod(job, HEADS)
             acc = acc_psum.tile([P, GROUP], F32, name="acc")
             chunk, place = divmod(head, 2)
             feats = slice(HEAD_DIM * place, HEAD_DIM * (place + 1))
-            for k_pass in range(K_PASSES):
-                nc.tensor.matmul_mx(
-                    out=acc[:],
-                    lhsT=w_codes[:, chunk, k_pass, feats].bitcast(FP8X4),
-                    lhsT_scale=w_scales[:, chunk, k_pass, feats],
-                    rhs=x_codes[group][:, k_pass, :].bitcast(FP8X4),
-                    rhs_scale=x_scales[group][:, k_pass, :],
-                    start=(k_pass == 0),
-                    stop=(k_pass == K_PASSES - 1),
-                )
+            parts = parts_of(group)
+            width = GROUP // parts
+            for part in range(parts):
+                for k_pass in range(K_PASSES):
+                    nc.tensor.matmul_mx(
+                        out=acc[:, width * part : width * (part + 1)],
+                        lhsT=w_codes[:, chunk, k_pass, feats].bitcast(FP8X4),
+                        lhsT_scale=w_scales[:, chunk, k_pass, feats],
+                        rhs=x_codes[group][:, part, k_pass, :].bitcast(FP8X4),
+                        rhs_scale=x_scales[group][:, part, k_pass, :],
+                        start=(k_pass == 0),
+                        stop=(k_pass == K_PASSES - 1),
+                    )
             return acc
 
-        def add_bias(acc, group, head):
-            biased[group, head] = biased_pool.tile([P, GROUP], F32, name="biased")
-            nc.scalar.activation(
-                out=biased[group, head][:], in_=acc[:], func=ACT.Identity, bias=b_col[:, head : head + 1], scale=1.0
-            )
+        def add_bias(job, acc, on_vector=False):
+            bias = b_col[:, job % HEADS : job % HEADS + 1]
+            biased[job] = biased_pool.tile([P, GROUP], F32, name="biased")
+            if on_vector:
+                nc.vector.tensor_scalar(out=biased[job][:], in0=acc[:], scalar1=bias, scalar2=None, op0=ALU.add)
+            else:
+                nc.scalar.activation(out=biased[job][:], in_=acc[:], func=ACT.Identity, bias=bias, scale=1.0)
 
-        def turn_back(group, t, bank):
+        def turn_back(unit):
+            first_job = unit // TILES * BANK_HEADS
+            t = unit % TILES
             u = turned_psum.tile([P, BANK_HEADS, HEAD_DIM], F32, name="u", tag="turned")
             for h in range(BANK_HEADS):
-                nc.tensor.transpose(
-                    u[:, h, :], biased[group, BANK_HEADS * bank + h][:, P * t : P * (t + 1)], sort_pairs[:]
-                )
+                nc.tensor.transpose(u[:, h, :], biased[first_job + h][:, P * t : P * (t + 1)], sort_pairs[:])
             return u
 
         def sum_squares(u):
@@ -219,50 +232,105 @@ def tile_selfattention_pa_t_kernel(tc, x, freqs, w, b, g, out):
                 )
             return prod
 
-        def add_pairs(prod, result_half):
+        def add_pairs(prod):
+            result = result_pool.tile([P, BANK_COLS], F32, name="result")
             nc.gpsimd.tensor_tensor(
-                out=result_half.rearrange("q (h f) -> q h f", h=BANK_HEADS),
+                out=result[:].rearrange("q (h f) -> q h f", h=BANK_HEADS),
                 in0=prod[:, :, 0, :],
                 in1=prod[:, :, 1, :],
                 op=ALU.add,
             )
+            return result
 
-        bank_cols = BANK_HEADS * HEAD_DIM
-        for i in range(-PROJECT_AHEAD, ALL_TILES):
-            ahead_group, head_pair = divmod(i + PROJECT_AHEAD, TILES)
-            projecting = ahead_group < GROUPS
-            finishing = i >= 0
-            block = i + QUANTISE_AHEAD
-            group, t = divmod(i, TILES)
+        padded_rows = keep.tile([P, P], BF16, name="padded_rows")
+        nc.vector.memset(padded_rows[:], 0.0)
+        b_col = keep.tile([P, HEADS], F32, name="b_col")
+        g_all = keep.tile([P, HEAD_DIM], F32, name="g_all")
 
-            if not finishing and head_pair + 1 < W_CHUNKS:
-                quantise_w_chunk(head_pair + 1)
-            if finishing:
-                u_0 = turn_back(group, t, 0)
-            if projecting:
-                acc_0 = project(ahead_group, 2 * head_pair)
-            if finishing:
-                u_1 = turn_back(group, t, 1)
-            if projecting:
-                acc_1 = project(ahead_group, 2 * head_pair + 1)
-            if finishing:
-                sums_0 = sum_squares(u_0)
-            if projecting:
-                add_bias(acc_0, ahead_group, 2 * head_pair)
-            if finishing:
-                rstd_0 = inverse_rms(sums_0)
-                sums_1 = sum_squares(u_1)
-            if projecting:
-                add_bias(acc_1, ahead_group, 2 * head_pair + 1)
-            if block < X_BLOCKS:
-                prepare_x_block(block)
-            if finishing:
-                rstd_1 = inverse_rms(sums_1)
-                matrix = matrices[:, group % SEQ_HALVES, t]
-                result = result_pool.tile([P, HEADS * HEAD_DIM], F32, name="result")
-                add_pairs(multiply(u_0, rstd_0, matrix), result[:, 0:bank_cols])
-            if block < X_BLOCKS and block % BLOCKS_PER_GROUP == BLOCKS_PER_GROUP - 1:
-                quantise_x_group(block // BLOCKS_PER_GROUP)
-            if finishing:
-                add_pairs(multiply(u_1, rstd_1, matrix), result[:, bank_cols : 2 * bank_cols])
-                nc.sync.dma_start(out=out_tiles[group, t], in_=result[:])
+        for k_pass in range(K_PASSES):
+            copy_block(*prepare_x_block(k_pass))
+        for k_pass in range(K_PASSES):
+            copy_block(*prepare_w_block(0, k_pass))
+        quantise_x(0, 0)
+        for k_pass in range(K_PASSES):
+            copy_block(*prepare_x_block(K_PASSES + k_pass))
+        quantise_w(0)
+        nc.vector.tensor_copy(out=padded_rows[0 : HEADS + 1, :], in_=small_rows[:])
+        for k_pass in range(K_PASSES):
+            copy_block(*prepare_w_block(1, k_pass))
+        b_turned = turned_psum.tile([P, P], BF16, name="b_turned", tag="turned")
+        nc.tensor.transpose(b_turned[:], padded_rows[:], ident_bf[:])
+        g_spread = turned_psum.tile([P, HEAD_DIM], F32, name="g_spread", tag="turned")
+        nc.tensor.matmul(
+            g_spread[:],
+            lhsT=ident_bf[:, G_ROW : G_ROW + 1].to_broadcast([P, P]),
+            rhs=padded_rows[:],
+            start=True,
+            stop=True,
+        )
+        quantise_x(0, 1)
+        nc.scalar.copy(out=b_col[:], in_=b_turned[:, 0:HEADS])
+        nc.scalar.copy(out=g_all[:], in_=g_spread[:])
+        quantise_w(1)
+        for job in range(BANK_HEADS):
+            add_bias(job, project(job), on_vector=job % 2 == 1)
+
+        matrices = keep.tile([P, SEQ_HALVES, TILES, 2, PAIRS, 2], F32, name="matrices")
+        for e in range(SEQ_HALVES):
+            for t in range(TILES):
+                nc.gpsimd.tensor_tensor(
+                    out=matrices[:, e, t],
+                    in0=freqs_sb[:, e, t, :].rearrange("q (j r i) -> q i j r", r=2, i=2),
+                    in1=g_all[:].rearrange("q (j i) -> q i j", i=2).unsqueeze(3).to_broadcast([P, 2, PAIRS, 2]),
+                    op=ALU.mult,
+                )
+
+        turns_at, blocks_at, jobs_at, biases_at, quantise_at = {}, {}, {}, {}, {}
+        for unit in range(UNITS):
+            turns_at.setdefault(unit - 1, []).append(unit)
+        for job in range(BANK_HEADS, UNITS):
+            jobs_at.setdefault(job - job % 2 - PROJECT_AHEAD, []).append(job)
+            biases_at.setdefault(job - BIAS_AHEAD, []).append(job)
+        for block in range(HALVES * BLOCKS_PER_GROUP, X_BLOCKS):
+            blocks_at.setdefault(max(3, 2 * block - X_BLOCK_LEAD), []).append((prepare_x_block, (block,)))
+        for group in range(2, GROUPS):
+            quantise_at[HEADS * group - X_QUANTISE_LEAD] = (quantise_x, (group, 0))
+        for c in range(2, W_CHUNKS):
+            blocks_at[c - 3] = [(prepare_w_block, (c, k_pass)) for k_pass in range(K_PASSES)]
+            quantise_at[c - 2] = (quantise_w, (c,))
+        for half in range(HALVES):
+            first = BLOCKS_PER_GROUP + K_PASSES * half
+            blocks_at[1 + half] = [(prepare_x_block, (first + k_pass,)) for k_pass in range(K_PASSES)]
+        quantise_at[3] = (quantise_x, (1, 0))
+        turns_at[3], turns_at[4] = [], [4, 5]
+        jobs_at.update({-2: [], 0: [], 1: [4, 5], 2: [6, 7], 4: [8, 9], 5: [10, 11]})
+        biases_at.update({-1: [], 0: [], 1: [], 2: [4, 5], 3: [6, 7], 4: [], 5: [8, 9], 6: [10, 11]})
+
+        turned = {}
+        accs = {}
+        waiting = []
+        for i in range(-1, UNITS):
+            for unit in turns_at.get(i, []):
+                turned[unit] = turn_back(unit)
+            ready, waiting = waiting, [prepare(*which) for prepare, which in blocks_at.get(i, [])]
+            if i >= 0:
+                sums = sum_squares(turned[i])
+            for job in biases_at.get(i, []):
+                add_bias(job, accs[job])
+            if i >= 0:
+                rstd = inverse_rms(sums)
+            for block in ready:
+                copy_block(*block)
+            for job in jobs_at.get(i, []):
+                accs[job] = project(job)
+            if i >= 0:
+                group, rest = divmod(i, HEADS)
+                bank, t = divmod(rest, TILES)
+                prod = multiply(turned[i], rstd, matrices[:, group % SEQ_HALVES, t])
+                result = add_pairs(prod)
+                nc.sync.dma_start(
+                    out=out_tiles[group, t][:, BANK_COLS * bank : BANK_COLS * (bank + 1)], in_=result[:]
+                )
+            if i in quantise_at:
+                quantise, which = quantise_at[i]
+                quantise(*which)

@@ -36,7 +36,7 @@ UNITS = GROUPS * BANKS * TILES
 PROJECT_AHEAD = 6
 BIAS_AHEAD = 5
 X_BLOCK_LEAD = 17
-X_QUANTISE_LEAD = 9
+X_QUANTISE_LEAD = 10
 G_ROW = HEADS
 
 FLOPS = 2 * TOKENS * K * HEADS * HEAD_DIM

@@ -62,7 +62,6 @@ def tile_selfattention_pa_t_kernel(tc, x, freqs, w, b, g, out):
         result_pool = ctx.enter_context(tc.tile_pool(name="result_pool", bufs=6))
         acc_psum = ctx.enter_context(tc.psum_pool(name="acc_psum", bufs=3))
         turned_psum = ctx.enter_context(tc.psum_pool(name="turned_psum", bufs=5))
-        ctx.enter_context(tc.manual_schedule())
 
         x_sb = keep.tile([P, GROUPS, TILES, K], BF16, name="x_sb")
         w_sb = keep.tile([P, HEADS, K], BF16, name="w_sb")
@@ -232,15 +231,13 @@ def tile_selfattention_pa_t_kernel(tc, x, freqs, w, b, g, out):
                 )
             return prod
 
-        def add_pairs(prod):
-            result = result_pool.tile([P, BANK_COLS], F32, name="result")
-            nc.gpsimd.tensor_tensor(
-                out=result[:].rearrange("q (h f) -> q h f", h=BANK_HEADS),
-                in0=prod[:, :, 0, :],
-                in1=prod[:, :, 1, :],
+        def add_pairs(engine, prod, result, heads):
+            engine.tensor_tensor(
+                out=result[:].rearrange("q (h f) -> q h f", h=BANK_HEADS)[:, heads, :],
+                in0=prod[:, heads, 0, :],
+                in1=prod[:, heads, 1, :],
                 op=ALU.add,
             )
-            return result
 
         padded_rows = keep.tile([P, P], BF16, name="padded_rows")
         nc.vector.memset(padded_rows[:], 0.0)
@@ -327,10 +324,16 @@ def tile_selfattention_pa_t_kernel(tc, x, freqs, w, b, g, out):
                 group, rest = divmod(i, HEADS)
                 bank, t = divmod(rest, TILES)
                 prod = multiply(turned[i], rstd, matrices[:, group % SEQ_HALVES, t])
-                result = add_pairs(prod)
-                nc.sync.dma_start(
-                    out=out_tiles[group, t][:, BANK_COLS * bank : BANK_COLS * (bank + 1)], in_=result[:]
-                )
+                result = result_pool.tile([P, BANK_COLS], F32, name="result")
+                columns = out_tiles[group, t][:, BANK_COLS * bank : BANK_COLS * (bank + 1)]
+                if i < UNITS - 1:
+                    add_pairs(nc.gpsimd, prod, result, slice(0, BANK_HEADS))
+                    nc.sync.dma_start(out=columns, in_=result[:])
+                else:
+                    for engine, queue, first in ((nc.gpsimd, nc.scalar, 0), (nc.vector, nc.sync, BANK_HEADS // 2)):
+                        add_pairs(engine, prod, result, slice(first, first + BANK_HEADS // 2))
+                        part = slice(HEAD_DIM * first, HEAD_DIM * (first + BANK_HEADS // 2))
+                        queue.dma_start(out=columns[:, part], in_=result[:, part])
             if i in quantise_at:
                 quantise, which = quantise_at[i]
                 quantise(*which)

@@ -303,6 +303,7 @@ def tile_selfattention_pa_t_kernel(tc, x, freqs, w, b, g, out):
         jobs_at.update({-2: [], 0: [], 1: [4, 5], 2: [6, 7], 4: [8, 9], 5: [10, 11]})
         biases_at.update({-1: [], 0: [], 1: [], 2: [4, 5], 3: [6, 7], 4: [], 5: [8, 9], 6: [10, 11]})
 
+        ctx.enter_context(tc.manual_schedule(engines={mybir.EngineType.DVE}))
         turned = {}
         accs = {}
         waiting = []

from contextlib import ExitStack

import concourse.mybir as mybir
from concourse.masks import make_identity

F32 = mybir.dt.float32
BF16 = mybir.dt.bfloat16
U32 = mybir.dt.uint32
U8 = mybir.dt.uint8
FP8X4 = mybir.dt.float8_e4m3fn_x4
ACT = mybir.ActivationFunctionType
ALU = mybir.AluOpType

P = 128
K = 1024
K_PASSES = 2
WORDS_PER_PASS = 256
HEADS = 8
HEAD_DIM = 128
PAIRS = HEAD_DIM // 2
EPS = 1e-6
TOKENS = 4096
GROUP = 512
GROUPS = TOKENS // GROUP
TILES = GROUP // P
SEQ_HALVES = 2
BLOCK_ROWS = 256
HALVES = GROUP // BLOCK_ROWS
BLOCKS_PER_GROUP = HALVES * K_PASSES
X_BLOCKS = GROUPS * BLOCKS_PER_GROUP
W_CHUNKS = HEADS * HEAD_DIM // BLOCK_ROWS
BANK_HEADS = 4
BANK_COLS = BANK_HEADS * HEAD_DIM
BANKS = HEADS // BANK_HEADS
UNITS = GROUPS * BANKS * TILES
PROJECT_AHEAD = 6
BIAS_AHEAD = 5
X_BLOCK_LEAD = 17
X_QUANTISE_LEAD = 10
G_ROW = HEADS

FLOPS = 2 * TOKENS * K * HEADS * HEAD_DIM


def tile_selfattention_pa_t_kernel(tc, x, freqs, w, b, g, out):
    nc = tc.nc
    x_groups = x.rearrange("n s k -> (n s) k").rearrange("(a q t) k -> a q t k", q=P, t=TILES)
    out_tiles = out.rearrange("n s h d -> (n s) (h d)").rearrange("(a q t) f -> a t q f", q=P, t=TILES)
    w_chunks = w.rearrange("(c r q) k -> c q r k", r=2, q=P)
    freqs_rows = freqs.rearrange("a s b j r i -> (a s b) (j r i)").rearrange(
        "(e q t) f -> q e t f", q=P, t=TILES
    )

    with ExitStack() as ctx:
        keep = ctx.enter_context(tc.tile_pool(name="keep", bufs=1))
        x_grouped_pool = ctx.enter_context(tc.tile_pool(name="x_grouped_pool", bufs=2))
        w_grouped_pool = ctx.enter_context(tc.tile_pool(name="w_grouped_pool", bufs=2))
        x_mx_pool = ctx.enter_context(tc.tile_pool(name="x_mx_pool", bufs=3))
        biased_pool = ctx.enter_context(tc.tile_pool(name="biased_pool", bufs=14))
        small_pool = ctx.enter_context(tc.tile_pool(name="small_pool", bufs=4))
        prod_pool = ctx.enter_context(tc.tile_pool(name="prod_pool", bufs=4))
        result_pool = ctx.enter_context(tc.tile_pool(name="result_pool", bufs=6))
        acc_psum = ctx.enter_context(tc.psum_pool(name="acc_psum", bufs=3))
        turned_psum = ctx.enter_context(tc.psum_pool(name="turned_psum", bufs=5))

        x_sb = keep.tile([P, GROUPS, TILES, K], BF16, name="x_sb")
        w_sb = keep.tile([P, HEADS, K], BF16, name="w_sb")
        small_rows = keep.tile([HEADS + 1, HEAD_DIM], BF16, name="small_rows")
        freqs_sb = keep.tile([P, SEQ_HALVES, TILES, 4 * PAIRS], BF16, name="freqs_sb")
        nc.scalar.dma_start(out=small_rows[0:HEADS, :], in_=b.rearrange("(h d) -> h d", d=HEAD_DIM))
        nc.scalar.dma_start(out=small_rows[G_ROW : G_ROW + 1, :], in_=g.unsqueeze(0))
        nc.sync.dma_start(out=x_sb[:, 0, 0:2], in_=x_groups[0][:, 0:2])
        nc.sync.dma_start(out=w_sb[:, 0:2, :], in_=w_chunks[0])
        nc.sync.dma_start(out=x_sb[:, 0, 2:4], in_=x_groups[0][:, 2:4])
        nc.sync.dma_start(out=w_sb[:, 2:4, :], in_=w_chunks[1])
        nc.sync.dma_start(out=freqs_sb[:], in_=freqs_rows)
        for c in range(2, W_CHUNKS):
            nc.sync.dma_start(out=w_sb[:, 2 * c : 2 * c + 2, :], in_=w_chunks[c])
        for a in range(1, GROUPS):
            nc.sync.dma_start(out=x_sb[:, a], in_=x_groups[a])

        warm = keep.tile([P, 1], F32, name="warm")
        nc.vector.memset(warm[:], 1.0)
        nc.scalar.activation(out=warm[:], in_=warm[:], func=ACT.Abs_reciprocal_sqrt)

        ident = keep.tile([P, P], F32, name="ident")
        make_identity(nc, ident[:])
        sort_pairs = keep.tile([P, P], F32, name="sort_pairs")
        nc.vector.tensor_copy(
            out=sort_pairs[:].rearrange("q (i j) -> q i j", i=2), in_=ident[:].rearrange("q (j i) -> q i j", i=2)
        )
        ident_bf = keep.tile([P, P], BF16, name="ident_bf")
        nc.vector.tensor_copy(out=ident_bf[:], in_=ident[:])

        def transpose_block(rows, k_pass):
            words = turned_psum.tile([P, 2, BLOCK_ROWS], F32, name="words", tag="turned")
            first = WORDS_PER_PASS * k_pass
            for u in range(2):
                for r in range(2):
                    nc.tensor.transpose(
                        words[:, u, P * r : P * (r + 1)],
                        rows[:, r, :].bitcast(F32)[:, first + u : first + WORDS_PER_PASS : 2],
                        ident[:],
                    )
            return words

        def copy_block(words, grouped, copy_out):
            copy_out(
                out=grouped.bitcast(F32).rearrange("q (n u) -> q n u", u=2),
                in_=words[:].rearrange("q u n -> q n u"),
            )

        x_grouped = {}
        x_codes = {}
        x_scales = {}

        def engine_of(k_pass):
            return nc.scalar.copy if k_pass == 0 else nc.vector.tensor_copy

        def parts_of(group):
            return HALVES if group == 0 else 1

        def prepare_x_block(block):
            group, rest = divmod(block, BLOCKS_PER_GROUP)
            half, k_pass = divmod(rest, K_PASSES)
            parts = parts_of(group)
            if rest == 0:
                x_grouped[group] = x_grouped_pool.tile(
                    [P, parts, K_PASSES, HALVES // parts, 4 * BLOCK_ROWS], BF16, name="x_grouped", align_bytes=64
                )
                x_codes[group] = x_mx_pool.tile(
                    [P, parts, K_PASSES, GROUP // parts], U32, name="x_codes", align_bytes=64
                )
                x_scales[group] = x_mx_pool.tile(
                    [P, parts, K_PASSES, GROUP // parts], U8, name="x_scales", align_bytes=64
                )
            part, place = (half, 0) if parts == HALVES else (0, half)
            words = transpose_block(x_sb[:, group, 2 * half : 2 * half + 2, :], k_pass)
            return words, x_grouped[group][:, part, k_pass, place, :], engine_of(k_pass)

        def quantise_x(group, part):
            nc.vector.quantize_mx(
                out=x_codes[group][:, part].rearrange("q c n -> q (c n)").bitcast(FP8X4),
                scales=x_scales[group][:, part].rearrange("q c n -> q (c n)"),
                in_=x_grouped[group][:, part].rearrange("q c e n -> q (c e n)"),
            )

        w_codes = keep.tile([P, W_CHUNKS, K_PASSES, BLOCK_ROWS], U32, name="w_codes", align_bytes=64)
        w_scales = keep.tile([P, W_CHUNKS, K_PASSES, BLOCK_ROWS], U8, name="w_scales", align_bytes=64)
        w_grouped = {}

        def prepare_w_block(c, k_pass):
            if k_pass == 0:
                w_grouped[c] = w_grouped_pool.tile(
                    [P, K_PASSES, 4 * BLOCK_ROWS], BF16, name="w_grouped", align_bytes=64
                )
            words = transpose_block(w_sb[:, 2 * c : 2 * c + 2, :], k_pass)
            return words, w_grouped[c][:, k_pass, :], engine_of(k_pass)

        def quantise_w(c):
            nc.vector.quantize_mx(
                out=w_codes[:, c].rearrange("q c n -> q (c n)").bitcast(FP8X4),
                scales=w_scales[:, c].rearrange("q c n -> q (c n)"),
                in_=w_grouped[c][:].rearrange("q c n -> q (c n)"),
            )

        biased = {}

        def project(job):
            group, head = divmod(job, HEADS)
            acc = acc_psum.tile([P, GROUP], F32, name="acc")
            chunk, place = divmod(head, 2)
            feats = slice(HEAD_DIM * place, HEAD_DIM * (place + 1))
            parts = parts_of(group)
            width = GROUP // parts
            for part in range(parts):
                for k_pass in range(K_PASSES):
                    nc.tensor.matmul_mx(
                        out=acc[:, width * part : width * (part + 1)],
                        lhsT=w_codes[:, chunk, k_pass, feats].bitcast(FP8X4),
                        lhsT_scale=w_scales[:, chunk, k_pass, feats],
                        rhs=x_codes[group][:, part, k_pass, :].bitcast(FP8X4),
                        rhs_scale=x_scales[group][:, part, k_pass, :],
                        start=(k_pass == 0),
                        stop=(k_pass == K_PASSES - 1),
                    )
            return acc

        def add_bias(job, acc, on_vector=False):
            bias = b_col[:, job % HEADS : job % HEADS + 1]
            biased[job] = biased_pool.tile([P, GROUP], F32, name="biased")
            if on_vector:
                nc.vector.tensor_scalar(out=biased[job][:], in0=acc[:], scalar1=bias, scalar2=None, op0=ALU.add)
            else:
                nc.scalar.activation(out=biased[job][:], in_=acc[:], func=ACT.Identity, bias=bias, scale=1.0)

        def turn_back(unit):
            first_job = unit // TILES * BANK_HEADS
            t = unit % TILES
            u = turned_psum.tile([P, BANK_HEADS, HEAD_DIM], F32, name="u", tag="turned")
            for h in range(BANK_HEADS):
                nc.tensor.transpose(u[:, h, :], biased[first_job + h][:, P * t : P * (t + 1)], sort_pairs[:])
            return u

        def sum_squares(u):
            sums = small_pool.tile([P, BANK_HEADS], F32, name="sums")
            squares = small_pool.tile([P, BANK_HEADS, HEAD_DIM], F32, name="squares")
            for h in range(BANK_HEADS):
                nc.scalar.activation(
                    out=squares[:, h, :], in_=u[:, h, :], func=ACT.Square, accum_out=sums[:, h : h + 1]
                )
            return sums

        def inverse_rms(sums):
            rstd = small_pool.tile([P, BANK_HEADS], F32, name="rstd")
            nc.scalar.activation(
                out=rstd[:], in_=sums[:], func=ACT.Abs_reciprocal_sqrt, scale=1.0 / HEAD_DIM, bias=EPS
            )
            return rstd

        def multiply(u, rstd, matrix):
            prod = prod_pool.tile([P, BANK_HEADS, 2, HEAD_DIM], F32, name="prod")
            for h in range(BANK_HEADS):
                nc.vector.scalar_tensor_tensor(
                    out=prod[:, h].rearrange("q i (j r) -> q (i j) r", r=2),
                    in0=u[:, h, :].unsqueeze(2).to_broadcast([P, HEAD_DIM, 2]),
                    scalar=rstd[:, h : h + 1],
                    in1=matrix.rearrange("q i j r -> q (i j) r"),
                    op0=ALU.mult,
                    op1=ALU.mult,
                )
            return prod

        def add_pairs(engine, prod, result, heads):
            engine.tensor_tensor(
                out=result[:].rearrange("q (h f) -> q h f", h=BANK_HEADS)[:, heads, :],
                in0=prod[:, heads, 0, :],
                in1=prod[:, heads, 1, :],
                op=ALU.add,
            )

        padded_rows = keep.tile([P, P], BF16, name="padded_rows")
        nc.vector.memset(padded_rows[:], 0.0)
        b_col = keep.tile([P, HEADS], F32, name="b_col")
        g_all = keep.tile([P, HEAD_DIM], F32, name="g_all")

        for k_pass in range(K_PASSES):
            copy_block(*prepare_x_block(k_pass))
        for k_pass in range(K_PASSES):
            copy_block(*prepare_w_block(0, k_pass))
        quantise_x(0, 0)
        for k_pass in range(K_PASSES):
            copy_block(*prepare_x_block(K_PASSES + k_pass))
        quantise_w(0)
        nc.vector.tensor_copy(out=padded_rows[0 : HEADS + 1, :], in_=small_rows[:])
        for k_pass in range(K_PASSES):
            copy_block(*prepare_w_block(1, k_pass))
        b_turned = turned_psum.tile([P, P], BF16, name="b_turned", tag="turned")
        nc.tensor.transpose(b_turned[:], padded_rows[:], ident_bf[:])
        g_spread = turned_psum.tile([P, HEAD_DIM], F32, name="g_spread", tag="turned")
        nc.tensor.matmul(
            g_spread[:],
            lhsT=ident_bf[:, G_ROW : G_ROW + 1].to_broadcast([P, P]),
            rhs=padded_rows[:],
            start=True,
            stop=True,
        )
        quantise_x(0, 1)
        nc.scalar.copy(out=b_col[:], in_=b_turned[:, 0:HEADS])
        nc.scalar.copy(out=g_all[:], in_=g_spread[:])
        quantise_w(1)
        for job in range(BANK_HEADS):
            add_bias(job, project(job), on_vector=job % 2 == 1)

        matrices = keep.tile([P, SEQ_HALVES, TILES, 2, PAIRS, 2], F32, name="matrices")
        for e in range(SEQ_HALVES):
            for t in range(TILES):
                nc.gpsimd.tensor_tensor(
                    out=matrices[:, e, t],
                    in0=freqs_sb[:, e, t, :].rearrange("q (j r i) -> q i j r", r=2, i=2),
                    in1=g_all[:].rearrange("q (j i) -> q i j", i=2).unsqueeze(3).to_broadcast([P, 2, PAIRS, 2]),
                    op=ALU.mult,
                )

        turns_at, blocks_at, jobs_at, biases_at, quantise_at = {}, {}, {}, {}, {}
        for unit in range(UNITS):
            turns_at.setdefault(unit - 1, []).append(unit)
        for job in range(BANK_HEADS, UNITS):
            jobs_at.setdefault(job - job % 2 - PROJECT_AHEAD, []).append(job)
            biases_at.setdefault(job - BIAS_AHEAD, []).append(job)
        for block in range(HALVES * BLOCKS_PER_GROUP, X_BLOCKS):
            blocks_at.setdefault(max(3, 2 * block - X_BLOCK_LEAD), []).append((prepare_x_block, (block,)))
        for group in range(2, GROUPS):
            quantise_at[HEADS * group - X_QUANTISE_LEAD] = (quantise_x, (group, 0))
        for c in range(2, W_CHUNKS):
            blocks_at[c - 3] = [(prepare_w_block, (c, k_pass)) for k_pass in range(K_PASSES)]
            quantise_at[c - 2] = (quantise_w, (c,))
        for half in range(HALVES):
            first = BLOCKS_PER_GROUP + K_PASSES * half
            blocks_at[1 + half] = [(prepare_x_block, (first + k_pass,)) for k_pass in range(K_PASSES)]
        quantise_at[3] = (quantise_x, (1, 0))
        turns_at[3], turns_at[4] = [], [4, 5]
        jobs_at.update({-2: [], 0: [], 1: [4, 5], 2: [6, 7], 4: [8, 9], 5: [10, 11]})
        biases_at.update({-1: [], 0: [], 1: [], 2: [4, 5], 3: [6, 7], 4: [], 5: [8, 9], 6: [10, 11]})

        ctx.enter_context(tc.manual_schedule(engines={mybir.EngineType.DVE}))
        turned = {}
        accs = {}
        waiting = []
        for i in range(-1, UNITS):
            for unit in turns_at.get(i, []):
                turned[unit] = turn_back(unit)
            ready, waiting = waiting, [prepare(*which) for prepare, which in blocks_at.get(i, [])]
            if i >= 0:
                sums = sum_squares(turned[i])
            for job in biases_at.get(i, []):
                add_bias(job, accs[job])
            if i >= 0:
                rstd = inverse_rms(sums)
            for block in ready:
                copy_block(*block)
            for job in jobs_at.get(i, []):
                accs[job] = project(job)
            if i >= 0:
                group, rest = divmod(i, HEADS)
                bank, t = divmod(rest, TILES)
                prod = multiply(turned[i], rstd, matrices[:, group % SEQ_HALVES, t])
                result = result_pool.tile([P, BANK_COLS], F32, name="result")
                columns = out_tiles[group, t][:, BANK_COLS * bank : BANK_COLS * (bank + 1)]
                if i < UNITS - 1:
                    add_pairs(nc.gpsimd, prod, result, slice(0, BANK_HEADS))
                    nc.sync.dma_start(out=columns, in_=result[:])
                else:
                    for engine, queue, first in ((nc.gpsimd, nc.scalar, 0), (nc.vector, nc.sync, BANK_HEADS // 2)):
                        add_pairs(engine, prod, result, slice(first, first + BANK_HEADS // 2))
                        part = slice(HEAD_DIM * first, HEAD_DIM * (first + BANK_HEADS // 2))
                        queue.dma_start(out=columns[:, part], in_=result[:, part])
            if i in quantise_at:
                quantise, which = quantise_at[i]
                quantise(*which)
